import numpy as np
import ml_dtypes


def mxq(x, axis, fmt="e4m3"):
    dtype, down = {"e4m3": (ml_dtypes.float8_e4m3fn, 7), "e5m2": (ml_dtypes.float8_e5m2, 14)}[fmt]
    v = np.moveaxis(np.asarray(x, np.float32).astype(ml_dtypes.bfloat16).astype(np.float64), axis, -1)
    blocks = v.reshape(v.shape[:-1] + (-1, 32))
    amax = np.abs(blocks).max(-1, keepdims=True)
    byte = np.maximum(np.where(amax > 0, np.frexp(amax)[1] - 1 + 127, 0) - down, 1)
    scale = np.exp2(byte - 127.0)
    codes = (blocks / scale).astype(np.float32).astype(dtype).astype(np.float64)
    return np.moveaxis((codes * scale).reshape(v.shape), -1, axis)


WIDE = False


def mx_kscale(k):
    if not WIDE:
        return np.ones(k)
    levels = np.array([10, -10, 5, -5, 0])
    a = np.random.permutation(np.resize(levels, k // 512 * 4)).reshape(k // 512, 4)
    idx = np.arange(k)
    return np.exp2(a[idx // 512, idx % 128 // 32])


BF16 = ml_dtypes.bfloat16


def bf(x):
    return np.asarray(x, np.float32).astype(BF16)


def f64(x):
    return np.asarray(x).astype(np.float64)


B, T, E, C, I, O = 32, 128, 4, 128, 512, 128


def setup_inputs():
    s = mx_kscale(I)
    return {
        'x': bf((np.random.standard_normal((B, T, E, I)) * s).reshape(B, T, E * I)),
        'combine_array': bf(np.random.uniform(size=(B, T, E, C)) * 4.0 / (C * np.sqrt(E))),
        'dispatch_mask': bf(np.random.uniform(size=(B, T, E, C)) * 1.7 / np.sqrt(T)),
        'weight': bf((np.random.standard_normal((O, E, I)) / np.sqrt(I) / s).reshape(O, E * I)),
        'bias': bf(np.random.standard_normal(O) * 0.25),
        'num_experts': E,
    }


def reference(x, combine_array, dispatch_mask, weight, bias, num_experts):
    x, combine_array, dispatch_mask, weight, bias = f64(x), f64(combine_array), f64(dispatch_mask), f64(weight), f64(bias)
    e = num_experts
    i = weight.shape[1] // e
    w = weight.reshape(e, -1, i)
    b = x.shape[0]
    xr = x.reshape(b, -1, e, i)
    xd = dispatch_mask.transpose(0, 2, 3, 1) @ xr.transpose(0, 2, 1, 3)
    y = (mxq(xd, 3, 'e4m3') @ mxq(w, 2, 'e4m3').transpose(0, 2, 1)) + bias
    k = e * y.shape[2]
    return mxq(combine_array.reshape(b, -1, k), 2, 'e4m3') @ mxq(y.reshape(b, k, -1), 1, 'e4m3')

@@ -1,0 +1,238 @@
+from contextlib import ExitStack
+
+import concourse.mybir as mybir
+from concourse.masks import make_identity
+
+F32 = mybir.dt.float32
+BF16 = mybir.dt.bfloat16
+U32 = mybir.dt.uint32
+U8 = mybir.dt.uint8
+FP8X4 = mybir.dt.float8_e4m3fn_x4
+ADD = mybir.AluOpType.add
+
+B, T, E, C, I, O = 32, 128, 4, 128, 512, 128
+P = 128
+NB = 2
+G = B // NB
+LA = 5
+FLOPS = 2 * B * E * C * I * T + 2 * B * E * C * I * O + 2 * B * T * E * C * O
+
+
+def tile_expertschoosemaskedexpand_t_kernel(
+    tc, x, combine_array, dispatch_mask, weight, bias, num_experts, out
+):
+    nc = tc.nc
+    assert num_experts == E
+    with ExitStack() as ctx:
+        const = ctx.enter_context(tc.tile_pool(name="const", bufs=1))
+        xin = ctx.enter_context(tc.tile_pool(name="xin", bufs=LA + 2))
+        dmin = ctx.enter_context(tc.tile_pool(name="dmin", bufs=LA + 2))
+        cbin = ctx.enter_context(tc.tile_pool(name="cbin", bufs=LA + 2))
+        work = ctx.enter_context(tc.tile_pool(name="work", bufs=3))
+        xd_pool = ctx.enter_context(tc.psum_pool(name="xdp", bufs=4))
+        ct_pool = ctx.enter_context(tc.psum_pool(name="ctp", bufs=1))
+        y_pool = ctx.enter_context(tc.psum_pool(name="yp", bufs=2))
+        o_pool = ctx.enter_context(tc.psum_pool(name="op", bufs=1))
+        ctx.enter_context(tc.manual_schedule())
+
+        x_t = {}
+        dm_t = {}
+        cb_t = {}
+        xg_t = {}
+        xc_t = {}
+        xs_t = {}
+        yc_t = {}
+        ycc_t = {}
+        ycs_t = {}
+        y_ps_t = {}
+        o_ps_t = {}
+
+        def load(g):
+            b0 = g * NB
+            dmt = dmin.tile([P, NB, E * C], BF16)
+            nc.sync.dma_start(
+                out=dmt[:], in_=dispatch_mask[b0 : b0 + NB].rearrange("b t e c -> t b (e c)")
+            )
+            xt = xin.tile([P, NB, E * I], BF16)
+            if g == 0:
+                for bb in range(NB):
+                    nc.sync.dma_start(out=xt[:, bb, :], in_=x[b0 + bb])
+            else:
+                nc.sync.dma_start(out=xt[:], in_=x[b0 : b0 + NB].rearrange("b t f -> t b f"))
+            cbt = cbin.tile([P, NB, E * C], BF16)
+            nc.sync.dma_start(
+                out=cbt[:], in_=combine_array[b0 : b0 + NB].rearrange("b t e c -> t b (e c)")
+            )
+            dm_t[g] = dmt
+            x_t[g] = xt
+            cb_t[g] = cbt
+
+        def copy_out(on_vector, dst, src):
+            if on_vector:
+                nc.vector.tensor_copy(out=dst, in_=src)
+            else:
+                nc.scalar.copy(out=dst, in_=src)
+
+        ident = const.tile([P, P], BF16)
+        make_identity(nc, ident[:])
+        ones = const.tile([P, P], BF16)
+        nc.vector.memset(ones[:], 1.0)
+        brow = const.tile([P, O], BF16)
+        nc.vector.memset(brow[:], 0.0)
+        nc.scalar.dma_start(out=brow[0:1, :], in_=bias.unsqueeze(0))
+
+        w_rows = weight.rearrange("a (q i) -> (a q) i", q=E).rearrange("(e o) i -> o e i", e=E)
+        w_raw = const.tile([P, E, I], BF16)
+        for h in range(2):
+            nc.sync.dma_start(out=w_raw[:, 2 * h : 2 * h + 2, :], in_=w_rows[:, 2 * h : 2 * h + 2, :])
+        for g in range(LA):
+            load(g)
+
+        w_grp = const.tile([P, E * O * 4], BF16, align_bytes=64)
+        w_codes = const.tile([P, E * O], U32, align_bytes=64)
+        w_scales = const.tile([P, E * O], U8, align_bytes=64)
+        for h in range(2):
+            w_ps = xd_pool.tile([P, 2, 4, O], BF16, name="xd_ps")
+            for ee in range(2):
+                for j in range(4):
+                    nc.tensor.transpose(
+                        out=w_ps[:, ee, j, :],
+                        in_=w_raw[:, 2 * h + ee, j * P : (j + 1) * P],
+                        identity=ident[:],
+                    )
+            copy_out(
+                h == 0,
+                w_grp[:, h * 1024 : (h + 1) * 1024].rearrange("p (e o j) -> p e o j", e=2, j=4),
+                w_ps[:].rearrange("p e j o -> p e o j"),
+            )
+        b_ps = o_pool.tile([P, NB, O], F32, name="o_ps")
+        nc.tensor.matmul(out=b_ps[:, 0, :], lhsT=ones[:], rhs=brow[:], start=True, stop=True)
+        bias_bc = const.tile([P, O], F32)
+        nc.vector.tensor_copy(out=bias_bc[:], in_=b_ps[:, 0, :])
+        nc.vector.quantize_mx(out=w_codes[:].bitcast(FP8X4), scales=w_scales[:], in_=w_grp[:])
+
+        def step1_bank(g, k, on_vector):
+            xd_ps = xd_pool.tile([P, 2, 4, C], BF16, name="xd_ps")
+            for u in range(2):
+                bb, e = divmod(2 * k + u, E)
+                for j in range(4):
+                    nc.tensor.matmul(
+                        out=xd_ps[:, u, j, :],
+                        lhsT=x_t[g][:, bb, e * I + j * P : e * I + (j + 1) * P],
+                        rhs=dm_t[g][:, bb, e * C : (e + 1) * C],
+                        start=True,
+                        stop=True,
+                    )
+            copy_out(
+                on_vector,
+                xg_t[g][:, k * 1024 : (k + 1) * 1024].rearrange("p (u c j) -> p u c j", u=2, j=4),
+                xd_ps[:].rearrange("p u j c -> p u c j"),
+            )
+
+        def comb_t(g):
+            ct_ps = ct_pool.tile([P, NB, E, T], BF16, name="ct_ps")
+            for bb in range(NB):
+                for e in range(E):
+                    nc.tensor.transpose(
+                        out=ct_ps[:, bb, e, :],
+                        in_=cb_t[g][:, bb, e * C : (e + 1) * C],
+                        identity=ident[:],
+                    )
+            copy_out(
+                False,
+                yc_t[g][:, NB * 512 :].rearrange("p (b t e) -> p b t e", b=NB, e=E),
+                ct_ps[:].rearrange("p b e t -> p b t e"),
+            )
+
+        def q1(g):
+            xc = work.tile([P, NB * E * C], U32, align_bytes=64)
+            xs = work.tile([P, NB * E * C], U8, align_bytes=64)
+            nc.vector.quantize_mx(out=xc[:].bitcast(FP8X4), scales=xs[:], in_=xg_t[g][:])
+            xc_t[g] = xc
+            xs_t[g] = xs
+
+        def p2(g):
+            for bb in range(NB):
+                y_ps = y_pool.tile([P, E, O], F32, name="y_ps")
+                for e in range(E):
+                    cols = slice((bb * E + e) * C, (bb * E + e + 1) * C)
+                    nc.tensor.matmul_mx(
+                        out=y_ps[:, e, :],
+                        lhsT=xc_t[g][:, cols].bitcast(FP8X4),
+                        lhsT_scale=xs_t[g][:, cols],
+                        rhs=w_codes[:, e * O : (e + 1) * O].bitcast(FP8X4),
+                        rhs_scale=w_scales[:, e * O : (e + 1) * O],
+                        start=True,
+                        stop=True,
+                    )
+                y_ps_t[(g, bb)] = y_ps
+
+        def y_exit(g):
+            for bb in range(NB):
+                nc.vector.tensor_tensor(
+                    out=yc_t[g][:, bb * 512 : (bb + 1) * 512].rearrange("p (o e) -> p o e", e=E),
+                    in0=y_ps_t[(g, bb)][:].rearrange("p e o -> p o e"),
+                    in1=bias_bc[:].unsqueeze(2).to_broadcast([P, O, E]),
+                    op=ADD,
+                )
+
+        def q2(g):
+            ycc = work.tile([P, NB * 256], U32, align_bytes=64)
+            ycs = work.tile([P, NB * 256], U8, align_bytes=64)
+            nc.vector.quantize_mx(out=ycc[:].bitcast(FP8X4), scales=ycs[:], in_=yc_t[g][:])
+            ycc_t[g] = ycc
+            ycs_t[g] = ycs
+
+        def p3(g):
+            o_ps = o_pool.tile([P, NB, O], F32, name="o_ps")
+            for bb in range(NB):
+                ycols = slice(bb * O, (bb + 1) * O)
+                ccols = slice(NB * O + bb * T, NB * O + (bb + 1) * T)
+                nc.tensor.matmul_mx(
+                    out=o_ps[:, bb, :],
+                    lhsT=ycc_t[g][:, ccols].bitcast(FP8X4),
+                    lhsT_scale=ycs_t[g][:, ccols],
+                    rhs=ycc_t[g][:, ycols].bitcast(FP8X4),
+                    rhs_scale=ycs_t[g][:, ycols],
+                    start=True,
+                    stop=True,
+                )
+            o_ps_t[g] = o_ps
+
+        def o_exit(g):
+            o_sb = work.tile([P, NB, O], F32)
+            nc.vector.tensor_copy(out=o_sb[:], in_=o_ps_t[g][:])
+            nc.sync.dma_start(
+                out=out[g * NB : (g + 1) * NB].rearrange("b t o -> t b o"), in_=o_sb[:]
+            )
+
+        for i in range(G + 2):
+            ga, gb, gc = i, i - 1, i - 2
+            has_a = ga < G
+            has_b = 0 <= gb < G
+            has_c = 0 <= gc < G
+            if has_b:
+                q1(gb)
+            if has_a:
+                if ga + LA < G:
+                    load(ga + LA)
+                xg = work.tile([P, NB * E * C * 4], BF16, align_bytes=64)
+                yc = work.tile([P, NB * 1024], BF16, align_bytes=64)
+                xg_t[ga] = xg
+                yc_t[ga] = yc
+                step1_bank(ga, 0, True)
+                step1_bank(ga, 1, False)
+                step1_bank(ga, 2, False)
+            if has_b:
+                p2(gb)
+            if has_c:
+                p3(gc)
+            if has_a:
+                step1_bank(ga, 3, False)
+                comb_t(ga)
+            if has_b:
+                y_exit(gb)
+            if has_c:
+                o_exit(gc)
+            if has_b:
+                q2(gb)

@@ -9,11 +9,11 @@ U32 = mybir.dt.uint32
 U8 = mybir.dt.uint8
 FP8X4 = mybir.dt.float8_e4m3fn_x4
 ADD = mybir.AluOpType.add
+MULT = mybir.AluOpType.mult
 
 B, T, E, C, I, O = 32, 128, 4, 128, 512, 128
 P = 128
-NB = 2
-G = B // NB
+SIZES = [2] * 15 + [1, 1]
 LA = 5
 FLOPS = 2 * B * E * C * I * T + 2 * B * E * C * I * O + 2 * B * T * E * C * O
 
@@ -23,12 +23,16 @@ def tile_expertschoosemaskedexpand_t_kernel(
 ):
     nc = tc.nc
     assert num_experts == E
+    assert sum(SIZES) == B
+    n_g = len(SIZES)
+    starts = [sum(SIZES[:g]) for g in range(n_g)]
     with ExitStack() as ctx:
         const = ctx.enter_context(tc.tile_pool(name="const", bufs=1))
-        xin = ctx.enter_context(tc.tile_pool(name="xin", bufs=LA + 2))
+        xin = ctx.enter_context(tc.tile_pool(name="xin", bufs=2 * (LA + 2)))
         dmin = ctx.enter_context(tc.tile_pool(name="dmin", bufs=LA + 2))
         cbin = ctx.enter_context(tc.tile_pool(name="cbin", bufs=LA + 2))
         work = ctx.enter_context(tc.tile_pool(name="work", bufs=3))
+        cgp = ctx.enter_context(tc.tile_pool(name="cgp", bufs=1))
         xd_pool = ctx.enter_context(tc.psum_pool(name="xdp", bufs=4))
         ct_pool = ctx.enter_context(tc.psum_pool(name="ctp", bufs=1))
         y_pool = ctx.enter_context(tc.psum_pool(name="yp", bufs=2))
@@ -44,27 +48,43 @@ def tile_expertschoosemaskedexpand_t_kernel(
         yc_t = {}
         ycc_t = {}
         ycs_t = {}
+        cg_t = {}
+        cc_t = {}
+        cs_t = {}
         y_ps_t = {}
         o_ps_t = {}
 
-        def load(g):
-            b0 = g * NB
-            dmt = dmin.tile([P, NB, E * C], BF16)
-            nc.sync.dma_start(
-                out=dmt[:], in_=dispatch_mask[b0 : b0 + NB].rearrange("b t e c -> t b (e c)")
-            )
-            xt = xin.tile([P, NB, E * I], BF16)
-            if g == 0:
-                for bb in range(NB):
-                    nc.sync.dma_start(out=xt[:, bb, :], in_=x[b0 + bb])
-            else:
-                nc.sync.dma_start(out=xt[:], in_=x[b0 : b0 + NB].rearrange("b t f -> t b f"))
-            cbt = cbin.tile([P, NB, E * C], BF16)
-            nc.sync.dma_start(
-                out=cbt[:], in_=combine_array[b0 : b0 + NB].rearrange("b t e c -> t b (e c)")
-            )
+        def load_dm_x(g):
+            b0 = starts[g]
+            nb = SIZES[g]
+            dmt = dmin.tile([P, nb, E * C], BF16)
             dm_t[g] = dmt
-            x_t[g] = xt
+            if g == 0:
+                for bb in range(nb):
+                    nc.sync.dma_start(
+                        out=dmt[:, bb, :], in_=dispatch_mask[b0 + bb].rearrange("t e c -> t (e c)")
+                    )
+                    xt = xin.tile([P, E * I], BF16)
+                    x_t[(g, bb)] = xt
+                    for h in range(2):
+                        cols = slice(h * 2 * I, (h + 1) * 2 * I)
+                        nc.sync.dma_start(out=xt[:, cols], in_=x[b0 + bb][:, cols])
+            else:
+                nc.sync.dma_start(
+                    out=dmt[:], in_=dispatch_mask[b0 : b0 + nb].rearrange("b t e c -> t b (e c)")
+                )
+                for bb in range(nb):
+                    xt = xin.tile([P, E * I], BF16)
+                    x_t[(g, bb)] = xt
+                    nc.sync.dma_start(out=xt[:], in_=x[b0 + bb])
+
+        def load_cb(g):
+            b0 = starts[g]
+            nb = SIZES[g]
+            cbt = cbin.tile([P, nb, E * C], BF16)
+            nc.sync.dma_start(
+                out=cbt[:], in_=combine_array[b0 : b0 + nb].rearrange("b t e c -> t b (e c)")
+            )
             cb_t[g] = cbt
 
         def copy_out(on_vector, dst, src):
@@ -81,35 +101,41 @@ def tile_expertschoosemaskedexpand_t_kernel(
         nc.vector.memset(brow[:], 0.0)
         nc.scalar.dma_start(out=brow[0:1, :], in_=bias.unsqueeze(0))
 
+        load_dm_x(0)
         w_rows = weight.rearrange("a (q i) -> (a q) i", q=E).rearrange("(e o) i -> o e i", e=E)
         w_raw = const.tile([P, E, I], BF16)
-        for h in range(2):
-            nc.sync.dma_start(out=w_raw[:, 2 * h : 2 * h + 2, :], in_=w_rows[:, 2 * h : 2 * h + 2, :])
-        for g in range(LA):
-            load(g)
+        nc.sync.dma_start(out=w_raw[:], in_=w_rows)
+        load_cb(0)
+        for g in range(1, LA):
+            load_dm_x(g)
+            load_cb(g)
 
         w_grp = const.tile([P, E * O * 4], BF16, align_bytes=64)
         w_codes = const.tile([P, E * O], U32, align_bytes=64)
         w_scales = const.tile([P, E * O], U8, align_bytes=64)
-        for h in range(2):
-            w_ps = xd_pool.tile([P, 2, 4, O], BF16, name="xd_ps")
-            for ee in range(2):
-                for j in range(4):
-                    nc.tensor.transpose(
-                        out=w_ps[:, ee, j, :],
-                        in_=w_raw[:, 2 * h + ee, j * P : (j + 1) * P],
-                        identity=ident[:],
-                    )
-            copy_out(
-                h == 0,
-                w_grp[:, h * 1024 : (h + 1) * 1024].rearrange("p (e o j) -> p e o j", e=2, j=4),
-                w_ps[:].rearrange("p e j o -> p e o j"),
-            )
-        b_ps = o_pool.tile([P, NB, O], F32, name="o_ps")
-        nc.tensor.matmul(out=b_ps[:, 0, :], lhsT=ones[:], rhs=brow[:], start=True, stop=True)
         bias_bc = const.tile([P, O], F32)
-        nc.vector.tensor_copy(out=bias_bc[:], in_=b_ps[:, 0, :])
-        nc.vector.quantize_mx(out=w_codes[:].bitcast(FP8X4), scales=w_scales[:], in_=w_grp[:])
+
+        def w_prep():
+            for h in range(2):
+                w_ps = xd_pool.tile([P, 2, 4, O], BF16, name="xd_ps")
+                for ee in range(2):
+                    for j in range(4):
+                        nc.tensor.transpose(
+                            out=w_ps[:, ee, j, :],
+                            in_=w_raw[:, 2 * h + ee, j * P : (j + 1) * P],
+                            identity=ident[:],
+                        )
+                copy_out(
+                    h == 0,
+                    w_grp[:, h * 1024 : (h + 1) * 1024].rearrange("p (e o j) -> p e o j", e=2, j=4),
+                    w_ps[:].rearrange("p e j o -> p e o j"),
+                )
+            b_ps = o_pool.tile([P, 2, O], F32, name="o_ps")
+            nc.tensor.matmul(out=b_ps[:, 0, :], lhsT=ones[:], rhs=brow[:], start=True, stop=True)
+            nc.vector.tensor_copy(out=bias_bc[:], in_=b_ps[:, 0, :])
+
+        def w_quant():
+            nc.vector.quantize_mx(out=w_codes[:].bitcast(FP8X4), scales=w_scales[:], in_=w_grp[:])
 
         def step1_bank(g, k, on_vector):
             xd_ps = xd_pool.tile([P, 2, 4, C], BF16, name="xd_ps")
@@ -118,7 +144,7 @@ def tile_expertschoosemaskedexpand_t_kernel(
                 for j in range(4):
                     nc.tensor.matmul(
                         out=xd_ps[:, u, j, :],
-                        lhsT=x_t[g][:, bb, e * I + j * P : e * I + (j + 1) * P],
+                        lhsT=x_t[(g, bb)][:, e * I + j * P : e * I + (j + 1) * P],
                         rhs=dm_t[g][:, bb, e * C : (e + 1) * C],
                         start=True,
                         stop=True,
@@ -130,29 +156,38 @@ def tile_expertschoosemaskedexpand_t_kernel(
             )
 
         def comb_t(g):
-            ct_ps = ct_pool.tile([P, NB, E, T], BF16, name="ct_ps")
-            for bb in range(NB):
+            nb = SIZES[g]
+            ct_ps = ct_pool.tile([P, nb, E, T], BF16, name="ct_ps")
+            for bb in range(nb):
                 for e in range(E):
                     nc.tensor.transpose(
                         out=ct_ps[:, bb, e, :],
                         in_=cb_t[g][:, bb, e * C : (e + 1) * C],
                         identity=ident[:],
                     )
-            copy_out(
-                False,
-                yc_t[g][:, NB * 512 :].rearrange("p (b t e) -> p b t e", b=NB, e=E),
-                ct_ps[:].rearrange("p b e t -> p b t e"),
+            ctmp = work.tile([P, nb * 512], BF16)
+            nc.scalar.copy(out=ctmp[:], in_=ct_ps[:].rearrange("p b e t -> p (b e t)"))
+            cg = cgp.tile([P, nb * 512], BF16, align_bytes=64)
+            nc.gpsimd.tensor_scalar(
+                out=cg[:].rearrange("p (b t e) -> p b t e", b=nb, e=E),
+                in0=ctmp[:].rearrange("p (b e t) -> p b t e", b=nb, e=E),
+                scalar1=1.0,
+                scalar2=0.0,
+                op0=MULT,
+                op1=ADD,
             )
+            cg_t[g] = cg
 
         def q1(g):
-            xc = work.tile([P, NB * E * C], U32, align_bytes=64)
-            xs = work.tile([P, NB * E * C], U8, align_bytes=64)
+            nb = SIZES[g]
+            xc = work.tile([P, nb * E * C], U32, align_bytes=64)
+            xs = work.tile([P, nb * E * C], U8, align_bytes=64)
             nc.vector.quantize_mx(out=xc[:].bitcast(FP8X4), scales=xs[:], in_=xg_t[g][:])
             xc_t[g] = xc
             xs_t[g] = xs
 
         def p2(g):
-            for bb in range(NB):
+            for bb in range(SIZES[g]):
                 y_ps = y_pool.tile([P, E, O], F32, name="y_ps")
                 for e in range(E):
                     cols = slice((bb * E + e) * C, (bb * E + e + 1) * C)
@@ -168,7 +203,7 @@ def tile_expertschoosemaskedexpand_t_kernel(
                 y_ps_t[(g, bb)] = y_ps
 
         def y_exit(g):
-            for bb in range(NB):
+            for bb in range(SIZES[g]):
                 nc.vector.tensor_tensor(
                     out=yc_t[g][:, bb * 512 : (bb + 1) * 512].rearrange("p (o e) -> p o e", e=E),
                     in0=y_ps_t[(g, bb)][:].rearrange("p e o -> p o e"),
@@ -177,21 +212,28 @@ def tile_expertschoosemaskedexpand_t_kernel(
                 )
 
         def q2(g):
-            ycc = work.tile([P, NB * 256], U32, align_bytes=64)
-            ycs = work.tile([P, NB * 256], U8, align_bytes=64)
+            nb = SIZES[g]
+            cc = work.tile([P, nb * 128], U32, align_bytes=64)
+            cs = work.tile([P, nb * 128], U8, align_bytes=64)
+            nc.vector.quantize_mx(out=cc[:].bitcast(FP8X4), scales=cs[:], in_=cg_t[g][:])
+            cc_t[g] = cc
+            cs_t[g] = cs
+            ycc = work.tile([P, nb * 128], U32, align_bytes=64)
+            ycs = work.tile([P, nb * 128], U8, align_bytes=64)
             nc.vector.quantize_mx(out=ycc[:].bitcast(FP8X4), scales=ycs[:], in_=yc_t[g][:])
             ycc_t[g] = ycc
             ycs_t[g] = ycs
 
         def p3(g):
-            o_ps = o_pool.tile([P, NB, O], F32, name="o_ps")
-            for bb in range(NB):
+            nb = SIZES[g]
+            o_ps = o_pool.tile([P, nb, O], F32, name="o_ps")
+            for bb in range(nb):
                 ycols = slice(bb * O, (bb + 1) * O)
-                ccols = slice(NB * O + bb * T, NB * O + (bb + 1) * T)
+                ccols = slice(bb * T, (bb + 1) * T)
                 nc.tensor.matmul_mx(
                     out=o_ps[:, bb, :],
-                    lhsT=ycc_t[g][:, ccols].bitcast(FP8X4),
-                    lhsT_scale=ycs_t[g][:, ccols],
+                    lhsT=cc_t[g][:, ccols].bitcast(FP8X4),
+                    lhsT_scale=cs_t[g][:, ccols],
                     rhs=ycc_t[g][:, ycols].bitcast(FP8X4),
                     rhs_scale=ycs_t[g][:, ycols],
                     start=True,
@@ -200,35 +242,44 @@ def tile_expertschoosemaskedexpand_t_kernel(
             o_ps_t[g] = o_ps
 
         def o_exit(g):
-            o_sb = work.tile([P, NB, O], F32)
-            nc.vector.tensor_copy(out=o_sb[:], in_=o_ps_t[g][:])
+            nb = SIZES[g]
+            o_sb = work.tile([P, nb, O], F32)
+            copy_out(False, o_sb[:], o_ps_t[g][:])
             nc.sync.dma_start(
-                out=out[g * NB : (g + 1) * NB].rearrange("b t o -> t b o"), in_=o_sb[:]
+                out=out[starts[g] : starts[g] + nb].rearrange("b t o -> t b o"), in_=o_sb[:]
             )
 
-        for i in range(G + 2):
+        for i in range(n_g + 2):
             ga, gb, gc = i, i - 1, i - 2
-            has_a = ga < G
-            has_b = 0 <= gb < G
-            has_c = 0 <= gc < G
+            has_a = ga < n_g
+            has_b = 0 <= gb < n_g
+            has_c = 0 <= gc < n_g
             if has_b:
                 q1(gb)
+            if i == 1:
+                w_quant()
             if has_a:
-                if ga + LA < G:
-                    load(ga + LA)
-                xg = work.tile([P, NB * E * C * 4], BF16, align_bytes=64)
-                yc = work.tile([P, NB * 1024], BF16, align_bytes=64)
+                if ga + LA < n_g:
+                    load_dm_x(ga + LA)
+                    load_cb(ga + LA)
+                nb = SIZES[ga]
+                xg = work.tile([P, nb * E * C * 4], BF16, align_bytes=64)
+                yc = work.tile([P, nb * 512], BF16, align_bytes=64)
                 xg_t[ga] = xg
                 yc_t[ga] = yc
-                step1_bank(ga, 0, True)
-                step1_bank(ga, 1, False)
-                step1_bank(ga, 2, False)
+                n_banks = 2 * nb
+                early = n_banks - 1 if nb == 2 else n_banks
+                for k in range(early):
+                    step1_bank(ga, k, k == 0 or (i == 0 and k == 2))
             if has_b:
                 p2(gb)
             if has_c:
                 p3(gc)
             if has_a:
-                step1_bank(ga, 3, False)
+                for k in range(early, n_banks):
+                    step1_bank(ga, k, False)
+                if i == 0:
+                    w_prep()
                 comb_t(ga)
             if has_b:
                 y_exit(gb)

@@ -267,20 +267,15 @@ def tile_expertschoosemaskedexpand_t_kernel(
                 yc = work.tile([P, nb * 512], BF16, align_bytes=64)
                 xg_t[ga] = xg
                 yc_t[ga] = yc
-                n_banks = 2 * nb
-                early = n_banks - 1 if nb == 2 else n_banks
-                for k in range(early):
+                for k in range(2 * nb):
                     step1_bank(ga, k, k == 0 or (i == 0 and k == 2))
+                if i == 0:
+                    w_prep()
+                comb_t(ga)
             if has_b:
                 p2(gb)
             if has_c:
                 p3(gc)
-            if has_a:
-                for k in range(early, n_banks):
-                    step1_bank(ga, k, False)
-                if i == 0:
-                    w_prep()
-                comb_t(ga)
             if has_b:
                 y_exit(gb)
             if has_c:

@@ -48,9 +48,7 @@ def tile_expertschoosemaskedexpand_t_kernel(
         yc_t = {}
         ycc_t = {}
         ycs_t = {}
-        cg_t = {}
-        cc_t = {}
-        cs_t = {}
+        ctmp_t = {}
         y_ps_t = {}
         o_ps_t = {}
 
@@ -167,22 +165,31 @@ def tile_expertschoosemaskedexpand_t_kernel(
                     )
             ctmp = work.tile([P, nb * 512], BF16)
             nc.scalar.copy(out=ctmp[:], in_=ct_ps[:].rearrange("p b e t -> p (b e t)"))
-            cg = cgp.tile([P, nb * 512], BF16, align_bytes=64)
+            ctmp_t[g] = ctmp
+
+        def regroup_comb(g):
+            nb = SIZES[g]
+            yc = cgp.tile([P, nb * 1024], BF16, align_bytes=64)
+            yc_t[g] = yc
             nc.gpsimd.tensor_scalar(
-                out=cg[:].rearrange("p (b t e) -> p b t e", b=nb, e=E),
-                in0=ctmp[:].rearrange("p (b e t) -> p b t e", b=nb, e=E),
+                out=yc[:, nb * 512 :].rearrange("p (b t e) -> p b t e", b=nb, e=E),
+                in0=ctmp_t[g][:].rearrange("p (b e t) -> p b t e", b=nb, e=E),
                 scalar1=1.0,
                 scalar2=0.0,
                 op0=MULT,
                 op1=ADD,
             )
-            cg_t[g] = cg
 
         def q1(g):
             nb = SIZES[g]
             xc = work.tile([P, nb * E * C], U32, align_bytes=64)
             xs = work.tile([P, nb * E * C], U8, align_bytes=64)
-            nc.vector.quantize_mx(out=xc[:].bitcast(FP8X4), scales=xs[:], in_=xg_t[g][:])
+            for bb in range(nb):
+                nc.vector.quantize_mx(
+                    out=xc[:, bb * 512 : (bb + 1) * 512].bitcast(FP8X4),
+                    scales=xs[:, bb * 512 : (bb + 1) * 512],
+                    in_=xg_t[g][:, bb * 2048 : (bb + 1) * 2048],
+                )
             xc_t[g] = xc
             xs_t[g] = xs
 
@@ -213,13 +220,8 @@ def tile_expertschoosemaskedexpand_t_kernel(
 
         def q2(g):
             nb = SIZES[g]
-            cc = work.tile([P, nb * 128], U32, align_bytes=64)
-            cs = work.tile([P, nb * 128], U8, align_bytes=64)
-            nc.vector.quantize_mx(out=cc[:].bitcast(FP8X4), scales=cs[:], in_=cg_t[g][:])
-            cc_t[g] = cc
-            cs_t[g] = cs
-            ycc = work.tile([P, nb * 128], U32, align_bytes=64)
-            ycs = work.tile([P, nb * 128], U8, align_bytes=64)
+            ycc = work.tile([P, nb * 256], U32, align_bytes=64)
+            ycs = work.tile([P, nb * 256], U8, align_bytes=64)
             nc.vector.quantize_mx(out=ycc[:].bitcast(FP8X4), scales=ycs[:], in_=yc_t[g][:])
             ycc_t[g] = ycc
             ycs_t[g] = ycs
@@ -229,11 +231,11 @@ def tile_expertschoosemaskedexpand_t_kernel(
             o_ps = o_pool.tile([P, nb, O], F32, name="o_ps")
             for bb in range(nb):
                 ycols = slice(bb * O, (bb + 1) * O)
-                ccols = slice(bb * T, (bb + 1) * T)
+                ccols = slice(nb * O + bb * T, nb * O + (bb + 1) * T)
                 nc.tensor.matmul_mx(
                     out=o_ps[:, bb, :],
-                    lhsT=cc_t[g][:, ccols].bitcast(FP8X4),
-                    lhsT_scale=cs_t[g][:, ccols],
+                    lhsT=ycc_t[g][:, ccols].bitcast(FP8X4),
+                    lhsT_scale=ycs_t[g][:, ccols],
                     rhs=ycc_t[g][:, ycols].bitcast(FP8X4),
                     rhs_scale=ycs_t[g][:, ycols],
                     start=True,
@@ -258,15 +260,17 @@ def tile_expertschoosemaskedexpand_t_kernel(
                 q1(gb)
             if i == 1:
                 w_quant()
+            if has_c:
+                q2(gc)
+            if has_b:
+                regroup_comb(gb)
             if has_a:
                 if ga + LA < n_g:
                     load_dm_x(ga + LA)
                     load_cb(ga + LA)
                 nb = SIZES[ga]
                 xg = work.tile([P, nb * E * C * 4], BF16, align_bytes=64)
-                yc = work.tile([P, nb * 512], BF16, align_bytes=64)
                 xg_t[ga] = xg
-                yc_t[ga] = yc
                 for k in range(2 * nb):
                     step1_bank(ga, k, k == 0 or (i == 0 and k == 2))
                 if i == 0:
@@ -280,5 +284,3 @@ def tile_expertschoosemaskedexpand_t_kernel(
                 y_exit(gb)
             if has_c:
                 o_exit(gc)
-            if has_b:
-                q2(gb)

@@ -32,7 +32,7 @@ def tile_expertschoosemaskedexpand_t_kernel(
         dmin = ctx.enter_context(tc.tile_pool(name="dmin", bufs=LA + 2))
         cbin = ctx.enter_context(tc.tile_pool(name="cbin", bufs=LA + 2))
         work = ctx.enter_context(tc.tile_pool(name="work", bufs=3))
-        cgp = ctx.enter_context(tc.tile_pool(name="cgp", bufs=1))
+        xga_pool = ctx.enter_context(tc.tile_pool(name="xga", bufs=1))
         xd_pool = ctx.enter_context(tc.psum_pool(name="xdp", bufs=4))
         ct_pool = ctx.enter_context(tc.psum_pool(name="ctp", bufs=1))
         y_pool = ctx.enter_context(tc.psum_pool(name="yp", bufs=2))
@@ -48,7 +48,6 @@ def tile_expertschoosemaskedexpand_t_kernel(
         yc_t = {}
         ycc_t = {}
         ycs_t = {}
-        ctmp_t = {}
         y_ps_t = {}
         o_ps_t = {}
 
@@ -79,9 +78,12 @@ def tile_expertschoosemaskedexpand_t_kernel(
         def load_cb(g):
             b0 = starts[g]
             nb = SIZES[g]
-            cbt = cbin.tile([P, nb, E * C], BF16)
+            cbt = cbin.tile([P, nb * 2, 2 * C], BF16)
             nc.sync.dma_start(
-                out=cbt[:], in_=combine_array[b0 : b0 + nb].rearrange("b t e c -> t b (e c)")
+                out=cbt[:],
+                in_=combine_array[b0 : b0 + nb].rearrange(
+                    "b (s tl) (h ep) c -> (tl h) (b s) (ep c)", s=2, h=2
+                ),
             )
             cb_t[g] = cbt
 
@@ -135,7 +137,12 @@ def tile_expertschoosemaskedexpand_t_kernel(
         def w_quant():
             nc.vector.quantize_mx(out=w_codes[:].bitcast(FP8X4), scales=w_scales[:], in_=w_grp[:])
 
-        def step1_bank(g, k, on_vector):
+        def xg_view(g, k):
+            return xg_t[(g, k // 2)][:, (k % 2) * 1024 : (k % 2 + 1) * 1024].rearrange(
+                "p (u c j) -> p u c j", u=2, j=4
+            )
+
+        def step1_bank(g, k, how):
             xd_ps = xd_pool.tile([P, 2, 4, C], BF16, name="xd_ps")
             for u in range(2):
                 bb, e = divmod(2 * k + u, E)
@@ -147,76 +154,67 @@ def tile_expertschoosemaskedexpand_t_kernel(
                         start=True,
                         stop=True,
                     )
-            copy_out(
-                on_vector,
-                xg_t[g][:, k * 1024 : (k + 1) * 1024].rearrange("p (u c j) -> p u c j", u=2, j=4),
-                xd_ps[:].rearrange("p u j c -> p u c j"),
-            )
+            if how == "gpsimd":
+                xtmp = work.tile([P, 1024], BF16)
+                nc.scalar.copy(out=xtmp[:], in_=xd_ps[:].rearrange("p u j c -> p (u j c)"))
+                nc.gpsimd.tensor_scalar(
+                    out=xg_view(g, k),
+                    in0=xtmp[:].rearrange("p (u j c) -> p u c j", u=2, j=4),
+                    scalar1=1.0,
+                    scalar2=0.0,
+                    op0=MULT,
+                    op1=ADD,
+                )
+            else:
+                copy_out(how == "vector", xg_view(g, k), xd_ps[:].rearrange("p u j c -> p u c j"))
 
         def comb_t(g):
             nb = SIZES[g]
-            ct_ps = ct_pool.tile([P, nb, E, T], BF16, name="ct_ps")
-            for bb in range(nb):
-                for e in range(E):
-                    nc.tensor.transpose(
-                        out=ct_ps[:, bb, e, :],
-                        in_=cb_t[g][:, bb, e * C : (e + 1) * C],
-                        identity=ident[:],
-                    )
-            ctmp = work.tile([P, nb * 512], BF16)
-            nc.scalar.copy(out=ctmp[:], in_=ct_ps[:].rearrange("p b e t -> p (b e t)"))
-            ctmp_t[g] = ctmp
-
-        def regroup_comb(g):
-            nb = SIZES[g]
-            yc = cgp.tile([P, nb * 1024], BF16, align_bytes=64)
-            yc_t[g] = yc
-            nc.gpsimd.tensor_scalar(
-                out=yc[:, nb * 512 :].rearrange("p (b t e) -> p b t e", b=nb, e=E),
-                in0=ctmp_t[g][:].rearrange("p (b e t) -> p b t e", b=nb, e=E),
-                scalar1=1.0,
-                scalar2=0.0,
-                op0=MULT,
-                op1=ADD,
+            ct_ps = ct_pool.tile([P, nb * 512], BF16, name="ct_ps")
+            for blk in range(nb * 4):
+                nc.tensor.transpose(
+                    out=ct_ps[:, blk * P : (blk + 1) * P],
+                    in_=cb_t[g][:, blk // 2, (blk % 2) * C : (blk % 2 + 1) * C],
+                    identity=ident[:],
+                )
+            nc.vector.tensor_copy(
+                out=yc_t[g][:].bitcast(F32)[:, nb * 256 :].rearrange(
+                    "p (g tl ep) -> p g tl ep", tl=64, ep=2
+                ),
+                in_=ct_ps[:].bitcast(F32).rearrange("p (g ep tl) -> p g tl ep", tl=64, ep=2),
             )
 
-        def q1(g):
-            nb = SIZES[g]
-            xc = work.tile([P, nb * E * C], U32, align_bytes=64)
-            xs = work.tile([P, nb * E * C], U8, align_bytes=64)
-            for bb in range(nb):
-                nc.vector.quantize_mx(
-                    out=xc[:, bb * 512 : (bb + 1) * 512].bitcast(FP8X4),
-                    scales=xs[:, bb * 512 : (bb + 1) * 512],
-                    in_=xg_t[g][:, bb * 2048 : (bb + 1) * 2048],
-                )
-            xc_t[g] = xc
-            xs_t[g] = xs
+        def q1(g, bb):
+            nc.vector.quantize_mx(
+                out=xc_t[g][:, bb * 512 : (bb + 1) * 512].bitcast(FP8X4),
+                scales=xs_t[g][:, bb * 512 : (bb + 1) * 512],
+                in_=xg_t[(g, bb)][:],
+            )
 
-        def p2(g):
-            for bb in range(SIZES[g]):
-                y_ps = y_pool.tile([P, E, O], F32, name="y_ps")
-                for e in range(E):
-                    cols = slice((bb * E + e) * C, (bb * E + e + 1) * C)
-                    nc.tensor.matmul_mx(
-                        out=y_ps[:, e, :],
-                        lhsT=xc_t[g][:, cols].bitcast(FP8X4),
-                        lhsT_scale=xs_t[g][:, cols],
-                        rhs=w_codes[:, e * O : (e + 1) * O].bitcast(FP8X4),
-                        rhs_scale=w_scales[:, e * O : (e + 1) * O],
-                        start=True,
-                        stop=True,
-                    )
-                y_ps_t[(g, bb)] = y_ps
-
-        def y_exit(g):
-            for bb in range(SIZES[g]):
-                nc.vector.tensor_tensor(
-                    out=yc_t[g][:, bb * 512 : (bb + 1) * 512].rearrange("p (o e) -> p o e", e=E),
-                    in0=y_ps_t[(g, bb)][:].rearrange("p e o -> p o e"),
-                    in1=bias_bc[:].unsqueeze(2).to_broadcast([P, O, E]),
-                    op=ADD,
+        def p2(g, bb):
+            y_ps = y_pool.tile([P, E, O], F32, name="y_ps")
+            for e in range(E):
+                cols = slice((bb * E + e) * C, (bb * E + e + 1) * C)
+                nc.tensor.matmul_mx(
+                    out=y_ps[:, e, :],
+                    lhsT=xc_t[g][:, cols].bitcast(FP8X4),
+                    lhsT_scale=xs_t[g][:, cols],
+                    rhs=w_codes[:, e * O : (e + 1) * O].bitcast(FP8X4),
+                    rhs_scale=w_scales[:, e * O : (e + 1) * O],
+                    start=True,
+                    stop=True,
                 )
+            y_ps_t[(g, bb)] = y_ps
+
+        def y_exit(g, bb):
+            nc.vector.tensor_tensor(
+                out=yc_t[g][:, bb * 512 : (bb + 1) * 512].rearrange(
+                    "p (o ep h) -> p o ep h", ep=2, h=2
+                ),
+                in0=y_ps_t[(g, bb)][:].rearrange("p (h ep) o -> p o ep h", h=2),
+                in1=bias_bc[:].unsqueeze(2).unsqueeze(3).to_broadcast([P, O, 2, 2]),
+                op=ADD,
+            )
 
         def q2(g):
             nb = SIZES[g]
@@ -246,7 +244,7 @@ def tile_expertschoosemaskedexpand_t_kernel(
         def o_exit(g):
             nb = SIZES[g]
             o_sb = work.tile([P, nb, O], F32)
-            copy_out(False, o_sb[:], o_ps_t[g][:])
+            copy_out(g % 2 == 0 and g < n_g - 3, o_sb[:], o_ps_t[g][:])
             nc.sync.dma_start(
                 out=out[starts[g] : starts[g] + nb].rearrange("b t o -> t b o"), in_=o_sb[:]
             )
@@ -256,31 +254,50 @@ def tile_expertschoosemaskedexpand_t_kernel(
             has_a = ga < n_g
             has_b = 0 <= gb < n_g
             has_c = 0 <= gc < n_g
-            if has_b:
-                q1(gb)
-            if i == 1:
-                w_quant()
             if has_c:
                 q2(gc)
             if has_b:
-                regroup_comb(gb)
+                nbb = SIZES[gb]
+                xc = work.tile([P, nbb * E * C], U32, align_bytes=64)
+                xs = work.tile([P, nbb * E * C], U8, align_bytes=64)
+                xc_t[gb] = xc
+                xs_t[gb] = xs
+                for bb in reversed(range(nbb)):
+                    q1(gb, bb)
+            if i == 1:
+                w_quant()
             if has_a:
                 if ga + LA < n_g:
                     load_dm_x(ga + LA)
                     load_cb(ga + LA)
                 nb = SIZES[ga]
-                xg = work.tile([P, nb * E * C * 4], BF16, align_bytes=64)
-                xg_t[ga] = xg
-                for k in range(2 * nb):
-                    step1_bank(ga, k, k == 0 or (i == 0 and k == 2))
+                yc = work.tile([P, nb * 1024], BF16, align_bytes=64)
+                yc_t[ga] = yc
+                if nb == 2:
+                    xga = xga_pool.tile([P, 2048], BF16, align_bytes=64)
+                    xgb = work.tile([P, 2048], BF16, align_bytes=64)
+                    xg_t[(ga, 0)] = xga
+                    xg_t[(ga, 1)] = xgb
+                    step1_bank(ga, 0, "gpsimd")
+                    step1_bank(ga, 2, "vector" if i == 0 else "scalar")
+                    step1_bank(ga, 3, "scalar")
+                    comb_t(ga)
+                    step1_bank(ga, 1, "scalar")
+                else:
+                    xgb = work.tile([P, 2048], BF16, align_bytes=64)
+                    xg_t[(ga, 0)] = xgb
+                    step1_bank(ga, 0, "vector")
+                    comb_t(ga)
+                    step1_bank(ga, 1, "scalar")
                 if i == 0:
                     w_prep()
-                comb_t(ga)
             if has_b:
-                p2(gb)
+                for bb in reversed(range(SIZES[gb])):
+                    p2(gb, bb)
             if has_c:
                 p3(gc)
             if has_b:
-                y_exit(gb)
+                for bb in reversed(range(SIZES[gb])):
+                    y_exit(gb, bb)
             if has_c:
                 o_exit(gc)

@@ -32,7 +32,8 @@ def tile_expertschoosemaskedexpand_t_kernel(
         dmin = ctx.enter_context(tc.tile_pool(name="dmin", bufs=LA + 2))
         cbin = ctx.enter_context(tc.tile_pool(name="cbin", bufs=LA + 2))
         work = ctx.enter_context(tc.tile_pool(name="work", bufs=3))
-        xga_pool = ctx.enter_context(tc.tile_pool(name="xga", bufs=1))
+        cgp = ctx.enter_context(tc.tile_pool(name="cgp", bufs=1))
+        osb = ctx.enter_context(tc.tile_pool(name="osb", bufs=len(SIZES)))
         xd_pool = ctx.enter_context(tc.psum_pool(name="xdp", bufs=4))
         ct_pool = ctx.enter_context(tc.psum_pool(name="ctp", bufs=1))
         y_pool = ctx.enter_context(tc.psum_pool(name="yp", bufs=2))
@@ -48,6 +49,7 @@ def tile_expertschoosemaskedexpand_t_kernel(
         yc_t = {}
         ycc_t = {}
         ycs_t = {}
+        ctmp_t = {}
         y_ps_t = {}
         o_ps_t = {}
 
@@ -78,12 +80,9 @@ def tile_expertschoosemaskedexpand_t_kernel(
         def load_cb(g):
             b0 = starts[g]
             nb = SIZES[g]
-            cbt = cbin.tile([P, nb * 2, 2 * C], BF16)
+            cbt = cbin.tile([P, nb, E * C], BF16)
             nc.sync.dma_start(
-                out=cbt[:],
-                in_=combine_array[b0 : b0 + nb].rearrange(
-                    "b (s tl) (h ep) c -> (tl h) (b s) (ep c)", s=2, h=2
-                ),
+                out=cbt[:], in_=combine_array[b0 : b0 + nb].rearrange("b t e c -> t b (e c)")
             )
             cb_t[g] = cbt
 
@@ -137,12 +136,7 @@ def tile_expertschoosemaskedexpand_t_kernel(
         def w_quant():
             nc.vector.quantize_mx(out=w_codes[:].bitcast(FP8X4), scales=w_scales[:], in_=w_grp[:])
 
-        def xg_view(g, k):
-            return xg_t[(g, k // 2)][:, (k % 2) * 1024 : (k % 2 + 1) * 1024].rearrange(
-                "p (u c j) -> p u c j", u=2, j=4
-            )
-
-        def step1_bank(g, k, how):
+        def step1_bank(g, k, on_vector):
             xd_ps = xd_pool.tile([P, 2, 4, C], BF16, name="xd_ps")
             for u in range(2):
                 bb, e = divmod(2 * k + u, E)
@@ -154,67 +148,76 @@ def tile_expertschoosemaskedexpand_t_kernel(
                         start=True,
                         stop=True,
                     )
-            if how == "gpsimd":
-                xtmp = work.tile([P, 1024], BF16)
-                nc.scalar.copy(out=xtmp[:], in_=xd_ps[:].rearrange("p u j c -> p (u j c)"))
-                nc.gpsimd.tensor_scalar(
-                    out=xg_view(g, k),
-                    in0=xtmp[:].rearrange("p (u j c) -> p u c j", u=2, j=4),
-                    scalar1=1.0,
-                    scalar2=0.0,
-                    op0=MULT,
-                    op1=ADD,
-                )
-            else:
-                copy_out(how == "vector", xg_view(g, k), xd_ps[:].rearrange("p u j c -> p u c j"))
+            copy_out(
+                on_vector,
+                xg_t[g][:, k * 1024 : (k + 1) * 1024].rearrange("p (u c j) -> p u c j", u=2, j=4),
+                xd_ps[:].rearrange("p u j c -> p u c j"),
+            )
 
         def comb_t(g):
             nb = SIZES[g]
-            ct_ps = ct_pool.tile([P, nb * 512], BF16, name="ct_ps")
-            for blk in range(nb * 4):
-                nc.tensor.transpose(
-                    out=ct_ps[:, blk * P : (blk + 1) * P],
-                    in_=cb_t[g][:, blk // 2, (blk % 2) * C : (blk % 2 + 1) * C],
-                    identity=ident[:],
+            ct_ps = ct_pool.tile([P, nb, E, T], BF16, name="ct_ps")
+            for bb in range(nb):
+                for e in range(E):
+                    nc.tensor.transpose(
+                        out=ct_ps[:, bb, e, :],
+                        in_=cb_t[g][:, bb, e * C : (e + 1) * C],
+                        identity=ident[:],
+                    )
+            ctmp = work.tile([P, nb * 512], BF16)
+            nc.scalar.copy(out=ctmp[:], in_=ct_ps[:].rearrange("p b e t -> p (b e t)"))
+            ctmp_t[g] = ctmp
+
+        def regroup_comb(g):
+            nb = SIZES[g]
+            yc = cgp.tile([P, nb * 1024], BF16, align_bytes=64)
+            yc_t[g] = yc
+            nc.gpsimd.tensor_scalar(
+                out=yc[:, nb * 512 :].rearrange("p (b t e) -> p b t e", b=nb, e=E),
+                in0=ctmp_t[g][:].rearrange("p (b e t) -> p b t e", b=nb, e=E),
+                scalar1=1.0,
+                scalar2=0.0,
+                op0=MULT,
+                op1=ADD,
+            )
+
+        def q1(g):
+            nb = SIZES[g]
+            xc = work.tile([P, nb * E * C], U32, align_bytes=64)
+            xs = work.tile([P, nb * E * C], U8, align_bytes=64)
+            for bb in range(nb):
+                nc.vector.quantize_mx(
+                    out=xc[:, bb * 512 : (bb + 1) * 512].bitcast(FP8X4),
+                    scales=xs[:, bb * 512 : (bb + 1) * 512],
+                    in_=xg_t[g][:, bb * 2048 : (bb + 1) * 2048],
                 )
-            nc.vector.tensor_copy(
-                out=yc_t[g][:].bitcast(F32)[:, nb * 256 :].rearrange(
-                    "p (g tl ep) -> p g tl ep", tl=64, ep=2
-                ),
-                in_=ct_ps[:].bitcast(F32).rearrange("p (g ep tl) -> p g tl ep", tl=64, ep=2),
-            )
+            xc_t[g] = xc
+            xs_t[g] = xs
 
-        def q1(g, bb):
-            nc.vector.quantize_mx(
-                out=xc_t[g][:, bb * 512 : (bb + 1) * 512].bitcast(FP8X4),
-                scales=xs_t[g][:, bb * 512 : (bb + 1) * 512],
-                in_=xg_t[(g, bb)][:],
-            )
+        def p2(g):
+            for bb in range(SIZES[g]):
+                y_ps = y_pool.tile([P, E, O], F32, name="y_ps")
+                for e in range(E):
+                    cols = slice((bb * E + e) * C, (bb * E + e + 1) * C)
+                    nc.tensor.matmul_mx(
+                        out=y_ps[:, e, :],
+                        lhsT=xc_t[g][:, cols].bitcast(FP8X4),
+                        lhsT_scale=xs_t[g][:, cols],
+                        rhs=w_codes[:, e * O : (e + 1) * O].bitcast(FP8X4),
+                        rhs_scale=w_scales[:, e * O : (e + 1) * O],
+                        start=True,
+                        stop=True,
+                    )
+                y_ps_t[(g, bb)] = y_ps
 
-        def p2(g, bb):
-            y_ps = y_pool.tile([P, E, O], F32, name="y_ps")
-            for e in range(E):
-                cols = slice((bb * E + e) * C, (bb * E + e + 1) * C)
-                nc.tensor.matmul_mx(
-                    out=y_ps[:, e, :],
-                    lhsT=xc_t[g][:, cols].bitcast(FP8X4),
-                    lhsT_scale=xs_t[g][:, cols],
-                    rhs=w_codes[:, e * O : (e + 1) * O].bitcast(FP8X4),
-                    rhs_scale=w_scales[:, e * O : (e + 1) * O],
-                    start=True,
-                    stop=True,
+        def y_exit(g):
+            for bb in range(SIZES[g]):
+                nc.vector.tensor_tensor(
+                    out=yc_t[g][:, bb * 512 : (bb + 1) * 512].rearrange("p (o e) -> p o e", e=E),
+                    in0=y_ps_t[(g, bb)][:].rearrange("p e o -> p o e"),
+                    in1=bias_bc[:].unsqueeze(2).to_broadcast([P, O, E]),
+                    op=ADD,
                 )
-            y_ps_t[(g, bb)] = y_ps
-
-        def y_exit(g, bb):
-            nc.vector.tensor_tensor(
-                out=yc_t[g][:, bb * 512 : (bb + 1) * 512].rearrange(
-                    "p (o ep h) -> p o ep h", ep=2, h=2
-                ),
-                in0=y_ps_t[(g, bb)][:].rearrange("p (h ep) o -> p o ep h", h=2),
-                in1=bias_bc[:].unsqueeze(2).unsqueeze(3).to_broadcast([P, O, 2, 2]),
-                op=ADD,
-            )
 
         def q2(g):
             nb = SIZES[g]
@@ -241,63 +244,55 @@ def tile_expertschoosemaskedexpand_t_kernel(
                 )
             o_ps_t[g] = o_ps
 
+        o_sb_t = {}
+        stored = []
+
         def o_exit(g):
             nb = SIZES[g]
-            o_sb = work.tile([P, nb, O], F32)
-            copy_out(g % 2 == 0 and g < n_g - 3, o_sb[:], o_ps_t[g][:])
-            nc.sync.dma_start(
-                out=out[starts[g] : starts[g] + nb].rearrange("b t o -> t b o"), in_=o_sb[:]
-            )
+            o_sb = osb.tile([P, nb, O], F32)
+            copy_out(False, o_sb[:], o_ps_t[g][:])
+            o_sb_t[g] = o_sb
+
+        def flush_stores(upto):
+            for g in range(len(stored), upto + 1):
+                nc.sync.dma_start(
+                    out=out[starts[g] : starts[g] + SIZES[g]].rearrange("b t o -> t b o"),
+                    in_=o_sb_t[g][:],
+                )
+                stored.append(g)
 
         for i in range(n_g + 2):
             ga, gb, gc = i, i - 1, i - 2
             has_a = ga < n_g
             has_b = 0 <= gb < n_g
             has_c = 0 <= gc < n_g
+            if has_b:
+                q1(gb)
+            if i == 1:
+                w_quant()
             if has_c:
                 q2(gc)
             if has_b:
-                nbb = SIZES[gb]
-                xc = work.tile([P, nbb * E * C], U32, align_bytes=64)
-                xs = work.tile([P, nbb * E * C], U8, align_bytes=64)
-                xc_t[gb] = xc
-                xs_t[gb] = xs
-                for bb in reversed(range(nbb)):
-                    q1(gb, bb)
-            if i == 1:
-                w_quant()
+                regroup_comb(gb)
             if has_a:
                 if ga + LA < n_g:
                     load_dm_x(ga + LA)
                     load_cb(ga + LA)
                 nb = SIZES[ga]
-                yc = work.tile([P, nb * 1024], BF16, align_bytes=64)
-                yc_t[ga] = yc
-                if nb == 2:
-                    xga = xga_pool.tile([P, 2048], BF16, align_bytes=64)
-                    xgb = work.tile([P, 2048], BF16, align_bytes=64)
-                    xg_t[(ga, 0)] = xga
-                    xg_t[(ga, 1)] = xgb
-                    step1_bank(ga, 0, "gpsimd")
-                    step1_bank(ga, 2, "vector" if i == 0 else "scalar")
-                    step1_bank(ga, 3, "scalar")
-                    comb_t(ga)
-                    step1_bank(ga, 1, "scalar")
-                else:
-                    xgb = work.tile([P, 2048], BF16, align_bytes=64)
-                    xg_t[(ga, 0)] = xgb
-                    step1_bank(ga, 0, "vector")
-                    comb_t(ga)
-                    step1_bank(ga, 1, "scalar")
+                xg = work.tile([P, nb * E * C * 4], BF16, align_bytes=64)
+                xg_t[ga] = xg
+                for k in range(2 * nb):
+                    step1_bank(ga, k, k == 0 or (i == 0 and k == 2))
                 if i == 0:
                     w_prep()
+                comb_t(ga)
             if has_b:
-                for bb in reversed(range(SIZES[gb])):
-                    p2(gb, bb)
+                p2(gb)
             if has_c:
                 p3(gc)
             if has_b:
-                for bb in reversed(range(SIZES[gb])):
-                    y_exit(gb, bb)
+                y_exit(gb)
             if has_c:
                 o_exit(gc)
+            if has_c and ga + LA >= n_g - 1:
+                flush_stores(gc)

@@ -81,9 +81,17 @@ def tile_expertschoosemaskedexpand_t_kernel(
             b0 = starts[g]
             nb = SIZES[g]
             cbt = cbin.tile([P, nb, E * C], BF16)
-            nc.sync.dma_start(
-                out=cbt[:], in_=combine_array[b0 : b0 + nb].rearrange("b t e c -> t b (e c)")
-            )
+            if nb == 2:
+                nc.sync.dma_start(
+                    out=cbt[:],
+                    in_=combine_array[b0 : b0 + nb]
+                    .rearrange("b t e c -> (b t) (e c)")
+                    .rearrange("(p r) k -> p r k", r=2),
+                )
+            else:
+                nc.sync.dma_start(
+                    out=cbt[:], in_=combine_array[b0 : b0 + nb].rearrange("b t e c -> t b (e c)")
+                )
             cb_t[g] = cbt
 
         def copy_out(on_vector, dst, src):
@@ -172,9 +180,10 @@ def tile_expertschoosemaskedexpand_t_kernel(
             nb = SIZES[g]
             yc = cgp.tile([P, nb * 1024], BF16, align_bytes=64)
             yc_t[g] = yc
+            regions = nb * E
             nc.gpsimd.tensor_scalar(
-                out=yc[:, nb * 512 :].rearrange("p (b t e) -> p b t e", b=nb, e=E),
-                in0=ctmp_t[g][:].rearrange("p (b e t) -> p b t e", b=nb, e=E),
+                out=yc[:, nb * 512 :].rearrange("p (q s) -> p q s", s=regions),
+                in0=ctmp_t[g][:].rearrange("p (s q) -> p q s", s=regions),
                 scalar1=1.0,
                 scalar2=0.0,
                 op0=MULT,

@@ -13,8 +13,11 @@ MULT = mybir.AluOpType.mult
 
 B, T, E, C, I, O = 32, 128, 4, 128, 512, 128
 P = 128
+PACK = 4
+UNIT = C * PACK
+BANK = 2 * UNIT
 SIZES = [2] * 15 + [1, 1]
-LA = 5
+AHEAD = 5
 FLOPS = 2 * B * E * C * I * T + 2 * B * E * C * I * O + 2 * B * T * E * C * O
 
 
@@ -24,75 +27,43 @@ def tile_expertschoosemaskedexpand_t_kernel(
     nc = tc.nc
     assert num_experts == E
     assert sum(SIZES) == B
-    n_g = len(SIZES)
-    starts = [sum(SIZES[:g]) for g in range(n_g)]
+    n_groups = len(SIZES)
+    first_batch = [sum(SIZES[:g]) for g in range(n_groups)]
+    n_paired = 2 * (len([s for s in SIZES if s == 2]) // 2)
+    units = [[g, g + 1] for g in range(0, n_paired, 2)] + [[g] for g in range(n_paired, n_groups)]
+    unit_of = {}
+    for u, members in enumerate(units):
+        for g in members:
+            unit_of[g] = u
+
     with ExitStack() as ctx:
         const = ctx.enter_context(tc.tile_pool(name="const", bufs=1))
-        xin = ctx.enter_context(tc.tile_pool(name="xin", bufs=2 * (LA + 2)))
-        dmin = ctx.enter_context(tc.tile_pool(name="dmin", bufs=LA + 2))
-        cbin = ctx.enter_context(tc.tile_pool(name="cbin", bufs=LA + 2))
+        x_pool = ctx.enter_context(tc.tile_pool(name="x_in", bufs=2 * (AHEAD + 2)))
+        mask_pool = ctx.enter_context(tc.tile_pool(name="mask_in", bufs=AHEAD + 2))
+        comb_pool = ctx.enter_context(tc.tile_pool(name="comb_in", bufs=AHEAD + 2))
         work = ctx.enter_context(tc.tile_pool(name="work", bufs=3))
-        cgp = ctx.enter_context(tc.tile_pool(name="cgp", bufs=1))
-        osb = ctx.enter_context(tc.tile_pool(name="osb", bufs=len(SIZES)))
-        xd_pool = ctx.enter_context(tc.psum_pool(name="xdp", bufs=4))
-        ct_pool = ctx.enter_context(tc.psum_pool(name="ctp", bufs=1))
-        y_pool = ctx.enter_context(tc.psum_pool(name="yp", bufs=2))
-        o_pool = ctx.enter_context(tc.psum_pool(name="op", bufs=1))
+        yc_pool = ctx.enter_context(tc.tile_pool(name="yc", bufs=1))
+        res_pool = ctx.enter_context(tc.tile_pool(name="res", bufs=len(units)))
+        xd_banks = ctx.enter_context(tc.psum_pool(name="xd_banks", bufs=4))
+        comb_bank = ctx.enter_context(tc.psum_pool(name="comb_bank", bufs=1))
+        y_banks = ctx.enter_context(tc.psum_pool(name="y_banks", bufs=2))
+        out_bank = ctx.enter_context(tc.psum_pool(name="out_bank", bufs=1))
         ctx.enter_context(tc.manual_schedule())
 
-        x_t = {}
-        dm_t = {}
-        cb_t = {}
-        xg_t = {}
-        xc_t = {}
-        xs_t = {}
-        yc_t = {}
-        ycc_t = {}
-        ycs_t = {}
-        ctmp_t = {}
-        y_ps_t = {}
-        o_ps_t = {}
-
-        def load_dm_x(g):
-            b0 = starts[g]
-            nb = SIZES[g]
-            dmt = dmin.tile([P, nb, E * C], BF16)
-            dm_t[g] = dmt
-            if g == 0:
-                for bb in range(nb):
-                    nc.sync.dma_start(
-                        out=dmt[:, bb, :], in_=dispatch_mask[b0 + bb].rearrange("t e c -> t (e c)")
-                    )
-                    xt = xin.tile([P, E * I], BF16)
-                    x_t[(g, bb)] = xt
-                    for h in range(2):
-                        cols = slice(h * 2 * I, (h + 1) * 2 * I)
-                        nc.sync.dma_start(out=xt[:, cols], in_=x[b0 + bb][:, cols])
-            else:
-                nc.sync.dma_start(
-                    out=dmt[:], in_=dispatch_mask[b0 : b0 + nb].rearrange("b t e c -> t b (e c)")
-                )
-                for bb in range(nb):
-                    xt = xin.tile([P, E * I], BF16)
-                    x_t[(g, bb)] = xt
-                    nc.sync.dma_start(out=xt[:], in_=x[b0 + bb])
-
-        def load_cb(g):
-            b0 = starts[g]
-            nb = SIZES[g]
-            cbt = cbin.tile([P, nb, E * C], BF16)
-            if nb == 2:
-                nc.sync.dma_start(
-                    out=cbt[:],
-                    in_=combine_array[b0 : b0 + nb]
-                    .rearrange("b t e c -> (b t) (e c)")
-                    .rearrange("(p r) k -> p r k", r=2),
-                )
-            else:
-                nc.sync.dma_start(
-                    out=cbt[:], in_=combine_array[b0 : b0 + nb].rearrange("b t e c -> t b (e c)")
-                )
-            cb_t[g] = cbt
+        x_of = {}
+        mask_of = {}
+        comb_of = {}
+        xd_grouped = {}
+        xd_codes = {}
+        xd_scales = {}
+        comb_rows = {}
+        yc_grouped = {}
+        yc_codes = {}
+        yc_scales = {}
+        y_bank_of = {}
+        out_bank_of = {}
+        result_of = {}
+        stored = []
 
         def copy_out(on_vector, dst, src):
             if on_vector:
@@ -100,208 +71,246 @@ def tile_expertschoosemaskedexpand_t_kernel(
             else:
                 nc.scalar.copy(out=dst, in_=src)
 
+        def load_mask_and_x(g):
+            b0 = first_batch[g]
+            nb = SIZES[g]
+            mask_sb = mask_pool.tile([P, nb, E * C], BF16)
+            mask_of[g] = mask_sb
+            if g == 0:
+                for bb in range(nb):
+                    nc.sync.dma_start(
+                        out=mask_sb[:, bb, :],
+                        in_=dispatch_mask[b0 + bb].rearrange("t e c -> t (e c)"),
+                    )
+                    x_sb = x_pool.tile([P, E * I], BF16)
+                    x_of[(g, bb)] = x_sb
+                    for half in range(2):
+                        cols = slice(half * 2 * I, (half + 1) * 2 * I)
+                        nc.sync.dma_start(out=x_sb[:, cols], in_=x[b0 + bb][:, cols])
+            else:
+                nc.sync.dma_start(
+                    out=mask_sb[:],
+                    in_=dispatch_mask[b0 : b0 + nb].rearrange("b t e c -> t b (e c)"),
+                )
+                for bb in range(nb):
+                    x_sb = x_pool.tile([P, E * I], BF16)
+                    x_of[(g, bb)] = x_sb
+                    nc.sync.dma_start(out=x_sb[:], in_=x[b0 + bb])
+
+        def load_comb(g):
+            b0 = first_batch[g]
+            nb = SIZES[g]
+            comb_sb = comb_pool.tile([P, nb, E * C], BF16)
+            nc.sync.dma_start(
+                out=comb_sb[:], in_=combine_array[b0 : b0 + nb].rearrange("b t e c -> t b (e c)")
+            )
+            comb_of[g] = comb_sb
+
         ident = const.tile([P, P], BF16)
         make_identity(nc, ident[:])
         ones = const.tile([P, P], BF16)
         nc.vector.memset(ones[:], 1.0)
-        brow = const.tile([P, O], BF16)
-        nc.vector.memset(brow[:], 0.0)
-        nc.scalar.dma_start(out=brow[0:1, :], in_=bias.unsqueeze(0))
+        bias_row = const.tile([P, O], BF16)
+        nc.vector.memset(bias_row[:], 0.0)
+        nc.scalar.dma_start(out=bias_row[0:1, :], in_=bias.unsqueeze(0))
 
-        load_dm_x(0)
+        load_mask_and_x(0)
         w_rows = weight.rearrange("a (q i) -> (a q) i", q=E).rearrange("(e o) i -> o e i", e=E)
-        w_raw = const.tile([P, E, I], BF16)
-        nc.sync.dma_start(out=w_raw[:], in_=w_rows)
-        load_cb(0)
-        for g in range(1, LA):
-            load_dm_x(g)
-            load_cb(g)
+        w_sb = const.tile([P, E, I], BF16)
+        nc.sync.dma_start(out=w_sb[:], in_=w_rows)
+        load_comb(0)
+        for g in range(1, AHEAD):
+            load_mask_and_x(g)
+            load_comb(g)
 
-        w_grp = const.tile([P, E * O * 4], BF16, align_bytes=64)
+        w_grouped = const.tile([P, E * UNIT], BF16, align_bytes=64)
         w_codes = const.tile([P, E * O], U32, align_bytes=64)
         w_scales = const.tile([P, E * O], U8, align_bytes=64)
-        bias_bc = const.tile([P, O], F32)
+        bias_all = const.tile([P, O], F32)
 
-        def w_prep():
-            for h in range(2):
-                w_ps = xd_pool.tile([P, 2, 4, O], BF16, name="xd_ps")
+        def prepare_w_and_bias():
+            for half in range(2):
+                w_ps = xd_banks.tile([P, 2, PACK, O], BF16, name="xd_ps")
                 for ee in range(2):
-                    for j in range(4):
+                    for j in range(PACK):
                         nc.tensor.transpose(
                             out=w_ps[:, ee, j, :],
-                            in_=w_raw[:, 2 * h + ee, j * P : (j + 1) * P],
+                            in_=w_sb[:, 2 * half + ee, j * P : (j + 1) * P],
                             identity=ident[:],
                         )
                 copy_out(
-                    h == 0,
-                    w_grp[:, h * 1024 : (h + 1) * 1024].rearrange("p (e o j) -> p e o j", e=2, j=4),
+                    half == 0,
+                    w_grouped[:, half * BANK : (half + 1) * BANK].rearrange(
+                        "p (e o j) -> p e o j", e=2, j=PACK
+                    ),
                     w_ps[:].rearrange("p e j o -> p e o j"),
                 )
-            b_ps = o_pool.tile([P, 2, O], F32, name="o_ps")
-            nc.tensor.matmul(out=b_ps[:, 0, :], lhsT=ones[:], rhs=brow[:], start=True, stop=True)
-            nc.vector.tensor_copy(out=bias_bc[:], in_=b_ps[:, 0, :])
+            bias_ps = out_bank.tile([P, O], F32, name="out_ps")
+            nc.tensor.matmul(out=bias_ps[:], lhsT=ones[:], rhs=bias_row[:], start=True, stop=True)
+            nc.vector.tensor_copy(out=bias_all[:], in_=bias_ps[:])
 
-        def w_quant():
-            nc.vector.quantize_mx(out=w_codes[:].bitcast(FP8X4), scales=w_scales[:], in_=w_grp[:])
+        def quantise_w():
+            nc.vector.quantize_mx(
+                out=w_codes[:].bitcast(FP8X4), scales=w_scales[:], in_=w_grouped[:]
+            )
 
         def step1_bank(g, k, on_vector):
-            xd_ps = xd_pool.tile([P, 2, 4, C], BF16, name="xd_ps")
+            xd_ps = xd_banks.tile([P, 2, PACK, C], BF16, name="xd_ps")
             for u in range(2):
                 bb, e = divmod(2 * k + u, E)
-                for j in range(4):
+                for j in range(PACK):
                     nc.tensor.matmul(
                         out=xd_ps[:, u, j, :],
-                        lhsT=x_t[(g, bb)][:, e * I + j * P : e * I + (j + 1) * P],
-                        rhs=dm_t[g][:, bb, e * C : (e + 1) * C],
+                        lhsT=x_of[(g, bb)][:, e * I + j * P : e * I + (j + 1) * P],
+                        rhs=mask_of[g][:, bb, e * C : (e + 1) * C],
                         start=True,
                         stop=True,
                     )
             copy_out(
                 on_vector,
-                xg_t[g][:, k * 1024 : (k + 1) * 1024].rearrange("p (u c j) -> p u c j", u=2, j=4),
+                xd_grouped[g][:, k * BANK : (k + 1) * BANK].rearrange(
+                    "p (u c j) -> p u c j", u=2, j=PACK
+                ),
                 xd_ps[:].rearrange("p u j c -> p u c j"),
             )
 
-        def comb_t(g):
+        def transpose_comb(g):
             nb = SIZES[g]
-            ct_ps = ct_pool.tile([P, nb, E, T], BF16, name="ct_ps")
+            comb_ps = comb_bank.tile([P, nb, E, T], BF16, name="comb_ps")
             for bb in range(nb):
                 for e in range(E):
                     nc.tensor.transpose(
-                        out=ct_ps[:, bb, e, :],
-                        in_=cb_t[g][:, bb, e * C : (e + 1) * C],
+                        out=comb_ps[:, bb, e, :],
+                        in_=comb_of[g][:, bb, e * C : (e + 1) * C],
                         identity=ident[:],
                     )
-            ctmp = work.tile([P, nb * 512], BF16)
-            nc.scalar.copy(out=ctmp[:], in_=ct_ps[:].rearrange("p b e t -> p (b e t)"))
-            ctmp_t[g] = ctmp
+            rows = work.tile([P, nb * UNIT], BF16)
+            nc.scalar.copy(out=rows[:], in_=comb_ps[:].rearrange("p b e t -> p (b e t)"))
+            comb_rows[g] = rows
 
         def regroup_comb(g):
             nb = SIZES[g]
-            yc = cgp.tile([P, nb * 1024], BF16, align_bytes=64)
-            yc_t[g] = yc
-            regions = nb * E
+            yc = yc_pool.tile([P, 2 * nb * UNIT], BF16, align_bytes=64)
+            yc_grouped[g] = yc
             nc.gpsimd.tensor_scalar(
-                out=yc[:, nb * 512 :].rearrange("p (q s) -> p q s", s=regions),
-                in0=ctmp_t[g][:].rearrange("p (s q) -> p q s", s=regions),
+                out=yc[:, nb * UNIT :].rearrange("p (b t e) -> p b t e", b=nb, e=E),
+                in0=comb_rows[g][:].rearrange("p (b e t) -> p b t e", b=nb, e=E),
                 scalar1=1.0,
                 scalar2=0.0,
                 op0=MULT,
                 op1=ADD,
             )
 
-        def q1(g):
+        def quantise_xd(g):
             nb = SIZES[g]
-            xc = work.tile([P, nb * E * C], U32, align_bytes=64)
-            xs = work.tile([P, nb * E * C], U8, align_bytes=64)
-            for bb in range(nb):
-                nc.vector.quantize_mx(
-                    out=xc[:, bb * 512 : (bb + 1) * 512].bitcast(FP8X4),
-                    scales=xs[:, bb * 512 : (bb + 1) * 512],
-                    in_=xg_t[g][:, bb * 2048 : (bb + 1) * 2048],
-                )
-            xc_t[g] = xc
-            xs_t[g] = xs
+            codes = work.tile([P, nb * E * C], U32, align_bytes=64)
+            scales = work.tile([P, nb * E * C], U8, align_bytes=64)
+            nc.vector.quantize_mx(
+                out=codes[:].bitcast(FP8X4), scales=scales[:], in_=xd_grouped[g][:]
+            )
+            xd_codes[g] = codes
+            xd_scales[g] = scales
 
-        def p2(g):
+        def step2(g):
             for bb in range(SIZES[g]):
-                y_ps = y_pool.tile([P, E, O], F32, name="y_ps")
+                y_ps = y_banks.tile([P, E, O], F32, name="y_ps")
                 for e in range(E):
                     cols = slice((bb * E + e) * C, (bb * E + e + 1) * C)
                     nc.tensor.matmul_mx(
                         out=y_ps[:, e, :],
-                        lhsT=xc_t[g][:, cols].bitcast(FP8X4),
-                        lhsT_scale=xs_t[g][:, cols],
+                        lhsT=xd_codes[g][:, cols].bitcast(FP8X4),
+                        lhsT_scale=xd_scales[g][:, cols],
                         rhs=w_codes[:, e * O : (e + 1) * O].bitcast(FP8X4),
                         rhs_scale=w_scales[:, e * O : (e + 1) * O],
                         start=True,
                         stop=True,
                     )
-                y_ps_t[(g, bb)] = y_ps
+                y_bank_of[(g, bb)] = y_ps
 
-        def y_exit(g):
+        def add_bias(g):
             for bb in range(SIZES[g]):
                 nc.vector.tensor_tensor(
-                    out=yc_t[g][:, bb * 512 : (bb + 1) * 512].rearrange("p (o e) -> p o e", e=E),
-                    in0=y_ps_t[(g, bb)][:].rearrange("p e o -> p o e"),
-                    in1=bias_bc[:].unsqueeze(2).to_broadcast([P, O, E]),
+                    out=yc_grouped[g][:, bb * UNIT : (bb + 1) * UNIT].rearrange(
+                        "p (o e) -> p o e", e=E
+                    ),
+                    in0=y_bank_of[(g, bb)][:].rearrange("p e o -> p o e"),
+                    in1=bias_all[:].unsqueeze(2).to_broadcast([P, O, E]),
                     op=ADD,
                 )
 
-        def q2(g):
+        def quantise_y_and_comb(g):
             nb = SIZES[g]
-            ycc = work.tile([P, nb * 256], U32, align_bytes=64)
-            ycs = work.tile([P, nb * 256], U8, align_bytes=64)
-            nc.vector.quantize_mx(out=ycc[:].bitcast(FP8X4), scales=ycs[:], in_=yc_t[g][:])
-            ycc_t[g] = ycc
-            ycs_t[g] = ycs
+            codes2 = work.tile([P, 2 * nb * O], U32, align_bytes=64)
+            scales2 = work.tile([P, 2 * nb * O], U8, align_bytes=64)
+            nc.vector.quantize_mx(
+                out=codes2[:].bitcast(FP8X4), scales=scales2[:], in_=yc_grouped[g][:]
+            )
+            yc_codes[g] = codes2
+            yc_scales[g] = scales2
 
-        def p3(g):
+        def step3(g):
             nb = SIZES[g]
-            o_ps = o_pool.tile([P, nb, O], F32, name="o_ps")
+            u = unit_of[g]
+            if g == units[u][0]:
+                out_ps = out_bank.tile([P, sum([SIZES[m] for m in units[u]]), O], F32, name="out_ps")
+                out_bank_of[u] = out_ps
             for bb in range(nb):
-                ycols = slice(bb * O, (bb + 1) * O)
-                ccols = slice(nb * O + bb * T, nb * O + (bb + 1) * T)
+                y_cols = slice(bb * O, (bb + 1) * O)
+                comb_cols = slice(nb * O + bb * T, nb * O + (bb + 1) * T)
                 nc.tensor.matmul_mx(
-                    out=o_ps[:, bb, :],
-                    lhsT=ycc_t[g][:, ccols].bitcast(FP8X4),
-                    lhsT_scale=ycs_t[g][:, ccols],
-                    rhs=ycc_t[g][:, ycols].bitcast(FP8X4),
-                    rhs_scale=ycs_t[g][:, ycols],
+                    out=out_bank_of[u][:, first_batch[g] - first_batch[units[u][0]] + bb, :],
+                    lhsT=yc_codes[g][:, comb_cols].bitcast(FP8X4),
+                    lhsT_scale=yc_scales[g][:, comb_cols],
+                    rhs=yc_codes[g][:, y_cols].bitcast(FP8X4),
+                    rhs_scale=yc_scales[g][:, y_cols],
                     start=True,
                     stop=True,
                 )
-            o_ps_t[g] = o_ps
 
-        o_sb_t = {}
-        stored = []
+        def result_out_of_psum(g):
+            u = unit_of[g]
+            if g == units[u][-1]:
+                result = res_pool.tile([P, sum([SIZES[m] for m in units[u]]), O], F32)
+                nc.scalar.copy(out=result[:], in_=out_bank_of[u][:])
+                result_of[u] = result
 
-        def o_exit(g):
-            nb = SIZES[g]
-            o_sb = osb.tile([P, nb, O], F32)
-            copy_out(False, o_sb[:], o_ps_t[g][:])
-            o_sb_t[g] = o_sb
-
-        def flush_stores(upto):
-            for g in range(len(stored), upto + 1):
+        def store_finished_units():
+            for u in range(len(stored), len(result_of)):
+                b0 = first_batch[units[u][0]]
+                nb = sum([SIZES[m] for m in units[u]])
                 nc.sync.dma_start(
-                    out=out[starts[g] : starts[g] + SIZES[g]].rearrange("b t o -> t b o"),
-                    in_=o_sb_t[g][:],
+                    out=out[b0 : b0 + nb].rearrange("b t o -> t b o"), in_=result_of[u][:]
                 )
-                stored.append(g)
+                stored.append(u)
 
-        for i in range(n_g + 2):
-            ga, gb, gc = i, i - 1, i - 2
-            has_a = ga < n_g
-            has_b = 0 <= gb < n_g
-            has_c = 0 <= gc < n_g
-            if has_b:
-                q1(gb)
-            if i == 1:
-                w_quant()
-            if has_c:
-                q2(gc)
-            if has_b:
-                regroup_comb(gb)
-            if has_a:
-                if ga + LA < n_g:
-                    load_dm_x(ga + LA)
-                    load_cb(ga + LA)
-                nb = SIZES[ga]
-                xg = work.tile([P, nb * E * C * 4], BF16, align_bytes=64)
-                xg_t[ga] = xg
-                for k in range(2 * nb):
-                    step1_bank(ga, k, k == 0 or (i == 0 and k == 2))
-                if i == 0:
-                    w_prep()
-                comb_t(ga)
-            if has_b:
-                p2(gb)
-            if has_c:
-                p3(gc)
-            if has_b:
-                y_exit(gb)
-            if has_c:
-                o_exit(gc)
-            if has_c and ga + LA >= n_g - 1:
-                flush_stores(gc)
+        for r in range(n_groups + 2):
+            g1, g2, g3 = r, r - 1, r - 2
+            if 0 <= g2 < n_groups:
+                quantise_xd(g2)
+            if r == 1:
+                quantise_w()
+            if 0 <= g3:
+                quantise_y_and_comb(g3)
+            if 0 <= g2 < n_groups:
+                regroup_comb(g2)
+            if g1 < n_groups:
+                if g1 + AHEAD < n_groups:
+                    load_mask_and_x(g1 + AHEAD)
+                    load_comb(g1 + AHEAD)
+                grouped = work.tile([P, SIZES[g1] * E * UNIT], BF16, align_bytes=64)
+                xd_grouped[g1] = grouped
+                for k in range(2 * SIZES[g1]):
+                    step1_bank(g1, k, k == 0 or (r == 0 and k == 2))
+                if r == 0:
+                    prepare_w_and_bias()
+                transpose_comb(g1)
+            if 0 <= g2 < n_groups:
+                step2(g2)
+            if 0 <= g3:
+                step3(g3)
+            if 0 <= g2 < n_groups:
+                add_bias(g2)
+            if 0 <= g3:
+                result_out_of_psum(g3)
+                if g1 + AHEAD >= n_groups - 1:
+                    store_finished_units()

from contextlib import ExitStack

import concourse.mybir as mybir
from concourse.masks import make_identity

F32 = mybir.dt.float32
BF16 = mybir.dt.bfloat16
U32 = mybir.dt.uint32
U8 = mybir.dt.uint8
FP8X4 = mybir.dt.float8_e4m3fn_x4
ADD = mybir.AluOpType.add
MULT = mybir.AluOpType.mult

B, T, E, C, I, O = 32, 128, 4, 128, 512, 128
P = 128
PACK = 4
UNIT = C * PACK
BANK = 2 * UNIT
SIZES = [2] * 15 + [1, 1]
AHEAD = 5
FLOPS = 2 * B * E * C * I * T + 2 * B * E * C * I * O + 2 * B * T * E * C * O


def tile_expertschoosemaskedexpand_t_kernel(
    tc, x, combine_array, dispatch_mask, weight, bias, num_experts, out
):
    nc = tc.nc
    assert num_experts == E
    assert sum(SIZES) == B
    n_groups = len(SIZES)
    first_batch = [sum(SIZES[:g]) for g in range(n_groups)]
    n_paired = 2 * (len([s for s in SIZES if s == 2]) // 2)
    units = [[g, g + 1] for g in range(0, n_paired, 2)] + [[g] for g in range(n_paired, n_groups)]
    unit_of = {}
    for u, members in enumerate(units):
        for g in members:
            unit_of[g] = u

    with ExitStack() as ctx:
        const = ctx.enter_context(tc.tile_pool(name="const", bufs=1))
        x_pool = ctx.enter_context(tc.tile_pool(name="x_in", bufs=2 * (AHEAD + 2)))
        mask_pool = ctx.enter_context(tc.tile_pool(name="mask_in", bufs=AHEAD + 2))
        comb_pool = ctx.enter_context(tc.tile_pool(name="comb_in", bufs=AHEAD + 2))
        work = ctx.enter_context(tc.tile_pool(name="work", bufs=3))
        yc_pool = ctx.enter_context(tc.tile_pool(name="yc", bufs=1))
        res_pool = ctx.enter_context(tc.tile_pool(name="res", bufs=len(units)))
        xd_banks = ctx.enter_context(tc.psum_pool(name="xd_banks", bufs=4))
        comb_bank = ctx.enter_context(tc.psum_pool(name="comb_bank", bufs=1))
        y_banks = ctx.enter_context(tc.psum_pool(name="y_banks", bufs=2))
        out_bank = ctx.enter_context(tc.psum_pool(name="out_bank", bufs=1))
        ctx.enter_context(tc.manual_schedule())

        x_of = {}
        mask_of = {}
        comb_of = {}
        xd_grouped = {}
        xd_codes = {}
        xd_scales = {}
        comb_rows = {}
        yc_grouped = {}
        yc_codes = {}
        yc_scales = {}
        y_bank_of = {}
        out_bank_of = {}
        result_of = {}
        stored = []

        def copy_out(on_vector, dst, src):
            if on_vector:
                nc.vector.tensor_copy(out=dst, in_=src)
            else:
                nc.scalar.copy(out=dst, in_=src)

        def load_mask_and_x(g):
            b0 = first_batch[g]
            nb = SIZES[g]
            mask_sb = mask_pool.tile([P, nb, E * C], BF16)
            mask_of[g] = mask_sb
            if g == 0:
                for bb in range(nb):
                    nc.sync.dma_start(
                        out=mask_sb[:, bb, :],
                        in_=dispatch_mask[b0 + bb].rearrange("t e c -> t (e c)"),
                    )
                    x_sb = x_pool.tile([P, E * I], BF16)
                    x_of[(g, bb)] = x_sb
                    for half in range(2):
                        cols = slice(half * 2 * I, (half + 1) * 2 * I)
                        nc.sync.dma_start(out=x_sb[:, cols], in_=x[b0 + bb][:, cols])
            else:
                nc.sync.dma_start(
                    out=mask_sb[:],
                    in_=dispatch_mask[b0 : b0 + nb].rearrange("b t e c -> t b (e c)"),
                )
                for bb in range(nb):
                    x_sb = x_pool.tile([P, E * I], BF16)
                    x_of[(g, bb)] = x_sb
                    nc.sync.dma_start(out=x_sb[:], in_=x[b0 + bb])

        def load_comb(g):
            b0 = first_batch[g]
            nb = SIZES[g]
            comb_sb = comb_pool.tile([P, nb, E * C], BF16)
            nc.sync.dma_start(
                out=comb_sb[:], in_=combine_array[b0 : b0 + nb].rearrange("b t e c -> t b (e c)")
            )
            comb_of[g] = comb_sb

        ident = const.tile([P, P], BF16)
        make_identity(nc, ident[:])
        ones = const.tile([P, P], BF16)
        nc.vector.memset(ones[:], 1.0)
        bias_row = const.tile([P, O], BF16)
        nc.vector.memset(bias_row[:], 0.0)
        nc.scalar.dma_start(out=bias_row[0:1, :], in_=bias.unsqueeze(0))

        load_mask_and_x(0)
        w_rows = weight.rearrange("a (q i) -> (a q) i", q=E).rearrange("(e o) i -> o e i", e=E)
        w_sb = const.tile([P, E, I], BF16)
        nc.sync.dma_start(out=w_sb[:], in_=w_rows)
        load_comb(0)
        for g in range(1, AHEAD):
            load_mask_and_x(g)
            load_comb(g)

        w_grouped = const.tile([P, E * UNIT], BF16, align_bytes=64)
        w_codes = const.tile([P, E * O], U32, align_bytes=64)
        w_scales = const.tile([P, E * O], U8, align_bytes=64)
        bias_all = const.tile([P, O], F32)

        def prepare_w_and_bias():
            for half in range(2):
                w_ps = xd_banks.tile([P, 2, PACK, O], BF16, name="xd_ps")
                for ee in range(2):
                    for j in range(PACK):
                        nc.tensor.transpose(
                            out=w_ps[:, ee, j, :],
                            in_=w_sb[:, 2 * half + ee, j * P : (j + 1) * P],
                            identity=ident[:],
                        )
                copy_out(
                    half == 0,
                    w_grouped[:, half * BANK : (half + 1) * BANK].rearrange(
                        "p (e o j) -> p e o j", e=2, j=PACK
                    ),
                    w_ps[:].rearrange("p e j o -> p e o j"),
                )
            bias_ps = out_bank.tile([P, O], F32, name="out_ps")
            nc.tensor.matmul(out=bias_ps[:], lhsT=ones[:], rhs=bias_row[:], start=True, stop=True)
            nc.vector.tensor_copy(out=bias_all[:], in_=bias_ps[:])

        def quantise_w():
            nc.vector.quantize_mx(
                out=w_codes[:].bitcast(FP8X4), scales=w_scales[:], in_=w_grouped[:]
            )

        def step1_bank(g, k, on_vector):
            xd_ps = xd_banks.tile([P, 2, PACK, C], BF16, name="xd_ps")
            for u in range(2):
                bb, e = divmod(2 * k + u, E)
                for j in range(PACK):
                    nc.tensor.matmul(
                        out=xd_ps[:, u, j, :],
                        lhsT=x_of[(g, bb)][:, e * I + j * P : e * I + (j + 1) * P],
                        rhs=mask_of[g][:, bb, e * C : (e + 1) * C],
                        start=True,
                        stop=True,
                    )
            copy_out(
                on_vector,
                xd_grouped[g][:, k * BANK : (k + 1) * BANK].rearrange(
                    "p (u c j) -> p u c j", u=2, j=PACK
                ),
                xd_ps[:].rearrange("p u j c -> p u c j"),
            )

        def transpose_comb(g):
            nb = SIZES[g]
            comb_ps = comb_bank.tile([P, nb, E, T], BF16, name="comb_ps")
            for bb in range(nb):
                for e in range(E):
                    nc.tensor.transpose(
                        out=comb_ps[:, bb, e, :],
                        in_=comb_of[g][:, bb, e * C : (e + 1) * C],
                        identity=ident[:],
                    )
            rows = work.tile([P, nb * UNIT], BF16)
            nc.scalar.copy(out=rows[:], in_=comb_ps[:].rearrange("p b e t -> p (b e t)"))
            comb_rows[g] = rows

        def regroup_comb(g):
            nb = SIZES[g]
            yc = yc_pool.tile([P, 2 * nb * UNIT], BF16, align_bytes=64)
            yc_grouped[g] = yc
            nc.gpsimd.tensor_scalar(
                out=yc[:, nb * UNIT :].rearrange("p (b t e) -> p b t e", b=nb, e=E),
                in0=comb_rows[g][:].rearrange("p (b e t) -> p b t e", b=nb, e=E),
                scalar1=1.0,
                scalar2=0.0,
                op0=MULT,
                op1=ADD,
            )

        def quantise_xd(g):
            nb = SIZES[g]
            codes = work.tile([P, nb * E * C], U32, align_bytes=64)
            scales = work.tile([P, nb * E * C], U8, align_bytes=64)
            nc.vector.quantize_mx(
                out=codes[:].bitcast(FP8X4), scales=scales[:], in_=xd_grouped[g][:]
            )
            xd_codes[g] = codes
            xd_scales[g] = scales

        def step2(g):
            for bb in range(SIZES[g]):
                y_ps = y_banks.tile([P, E, O], F32, name="y_ps")
                for e in range(E):
                    cols = slice((bb * E + e) * C, (bb * E + e + 1) * C)
                    nc.tensor.matmul_mx(
                        out=y_ps[:, e, :],
                        lhsT=xd_codes[g][:, cols].bitcast(FP8X4),
                        lhsT_scale=xd_scales[g][:, cols],
                        rhs=w_codes[:, e * O : (e + 1) * O].bitcast(FP8X4),
                        rhs_scale=w_scales[:, e * O : (e + 1) * O],
                        start=True,
                        stop=True,
                    )
                y_bank_of[(g, bb)] = y_ps

        def add_bias(g):
            for bb in range(SIZES[g]):
                nc.vector.tensor_tensor(
                    out=yc_grouped[g][:, bb * UNIT : (bb + 1) * UNIT].rearrange(
                        "p (o e) -> p o e", e=E
                    ),
                    in0=y_bank_of[(g, bb)][:].rearrange("p e o -> p o e"),
                    in1=bias_all[:].unsqueeze(2).to_broadcast([P, O, E]),
                    op=ADD,
                )

        def quantise_y_and_comb(g):
            nb = SIZES[g]
            codes2 = work.tile([P, 2 * nb * O], U32, align_bytes=64)
            scales2 = work.tile([P, 2 * nb * O], U8, align_bytes=64)
            nc.vector.quantize_mx(
                out=codes2[:].bitcast(FP8X4), scales=scales2[:], in_=yc_grouped[g][:]
            )
            yc_codes[g] = codes2
            yc_scales[g] = scales2

        def step3(g):
            nb = SIZES[g]
            u = unit_of[g]
            if g == units[u][0]:
                out_ps = out_bank.tile([P, sum([SIZES[m] for m in units[u]]), O], F32, name="out_ps")
                out_bank_of[u] = out_ps
            for bb in range(nb):
                y_cols = slice(bb * O, (bb + 1) * O)
                comb_cols = slice(nb * O + bb * T, nb * O + (bb + 1) * T)
                nc.tensor.matmul_mx(
                    out=out_bank_of[u][:, first_batch[g] - first_batch[units[u][0]] + bb, :],
                    lhsT=yc_codes[g][:, comb_cols].bitcast(FP8X4),
                    lhsT_scale=yc_scales[g][:, comb_cols],
                    rhs=yc_codes[g][:, y_cols].bitcast(FP8X4),
                    rhs_scale=yc_scales[g][:, y_cols],
                    start=True,
                    stop=True,
                )

        def result_out_of_psum(g):
            u = unit_of[g]
            if g == units[u][-1]:
                result = res_pool.tile([P, sum([SIZES[m] for m in units[u]]), O], F32)
                nc.scalar.copy(out=result[:], in_=out_bank_of[u][:])
                result_of[u] = result

        def store_finished_units():
            for u in range(len(stored), len(result_of)):
                b0 = first_batch[units[u][0]]
                nb = sum([SIZES[m] for m in units[u]])
                nc.sync.dma_start(
                    out=out[b0 : b0 + nb].rearrange("b t o -> t b o"), in_=result_of[u][:]
                )
                stored.append(u)

        for r in range(n_groups + 2):
            g1, g2, g3 = r, r - 1, r - 2
            if 0 <= g2 < n_groups:
                quantise_xd(g2)
            if r == 1:
                quantise_w()
            if 0 <= g3:
                quantise_y_and_comb(g3)
            if 0 <= g2 < n_groups:
                regroup_comb(g2)
            if g1 < n_groups:
                if g1 + AHEAD < n_groups:
                    load_mask_and_x(g1 + AHEAD)
                    load_comb(g1 + AHEAD)
                grouped = work.tile([P, SIZES[g1] * E * UNIT], BF16, align_bytes=64)
                xd_grouped[g1] = grouped
                for k in range(2 * SIZES[g1]):
                    step1_bank(g1, k, k == 0 or (r == 0 and k == 2))
                if r == 0:
                    prepare_w_and_bias()
                transpose_comb(g1)
            if 0 <= g2 < n_groups:
                step2(g2)
            if 0 <= g3:
                step3(g3)
            if 0 <= g2 < n_groups:
                add_bias(g2)
            if 0 <= g3:
                result_out_of_psum(g3)
                if g1 + AHEAD >= n_groups - 1:
                    store_finished_units()
